import numpy as np
import ml_dtypes

BF16 = ml_dtypes.bfloat16


def bf(x):
    return np.asarray(x, np.float32).astype(BF16)


def f32(x):
    return np.asarray(x, np.float32)


def f64(x):
    return np.asarray(x).astype(np.float64)


def striped(idx):
    return np.tile(idx.reshape(-1, 16).T, (8, 1))


C, S, N, H = 1024, 512, 384, 256


def setup_inputs():
    return {"x": f32(np.random.standard_normal((C, S))), "hid": bf(np.abs(np.random.standard_normal((H, C)))), "w_s": bf(0.5 * np.random.standard_normal((H, N)) / np.sqrt(H)), "w_t": bf(np.random.standard_normal((H, N)) / np.sqrt(H)), "offs": striped(np.random.permutation(S)[:N])}


def reference(x, hid, w_s, w_t, offs):
    idx = offs[:16].T.reshape(-1)
    sc = f64(hid).T @ f64(w_s)
    tr = f64(hid).T @ f64(w_t)
    return f64(x)[:, idx] * np.exp(sc) + tr

@@ -1,0 +1,65 @@
+import concourse.mybir as mybir
+
+P = 128
+C, S, N, H = 1024, 512, 384, 256
+BLOCKS = C // P
+KSTEPS = H // P
+
+BF16, F32, U16 = mybir.dt.bfloat16, mybir.dt.float32, mybir.dt.uint16
+MULT, ADD = mybir.AluOpType.mult, mybir.AluOpType.add
+EXP = mybir.ActivationFunctionType.Exp
+
+FLOPS = 2 * 2 * C * H * N
+BYTES = 4 * C * N + 2 * H * C + 2 * 2 * H * N + 2 * P * (N // 16) + 4 * C * N
+
+
+def tile_affine_coupling_layer_kernel(tc, x, hid, w_s, w_t, offs, out):
+    nc = tc.nc
+    with (
+        tc.tile_pool(name="held", bufs=1) as held,
+        tc.tile_pool(name="work", bufs=3) as work,
+        tc.psum_pool(name="psum", bufs=4) as psum,
+    ):
+        offsets = held.tile([P, N // 16], U16, name="offsets")
+        nc.sync.dma_start(offsets[:], offs)
+
+        ws_sb = held.tile([P, KSTEPS, N], BF16, name="ws_sb")
+        wt_sb = held.tile([P, KSTEPS, N], BF16, name="wt_sb")
+        hid_sb = held.tile([P, KSTEPS, C], BF16, name="hid_sb")
+        nc.scalar.dma_start(hid_sb[:], hid.rearrange("(k p) c -> p k c", p=P))
+        nc.sync.dma_start(ws_sb[:], w_s.rearrange("(k p) n -> p k n", p=P))
+        nc.scalar.dma_start(wt_sb[:], w_t.rearrange("(k p) n -> p k n", p=P))
+
+        x_blocks = x.rearrange("(b p) s -> b p s", p=P)
+        out_blocks = out.rearrange("(b p) n -> b p n", p=P)
+        x_sb = []
+        for b in range(BLOCKS):
+            x_b = held.tile([P, S], F32, name=f"x{b}")
+            nc.sync.dma_start(x_b[:], x_blocks[b])
+            x_sb.append(x_b)
+
+        for b in range(BLOCKS):
+            samples = slice(b * P, (b + 1) * P)
+
+            sc = psum.tile([P, N], F32, name="sc")
+            tr = psum.tile([P, N], F32, name="tr")
+            for acc, w_sb in ((sc, ws_sb), (tr, wt_sb)):
+                for k in range(KSTEPS):
+                    nc.tensor.matmul(
+                        acc[:],
+                        hid_sb[:, k, samples],
+                        w_sb[:, k, :],
+                        start=(k == 0),
+                        stop=(k == KSTEPS - 1),
+                    )
+
+            scale = work.tile([P, N], F32, name="scale")
+            nc.scalar.activation(scale[:], sc[:], EXP)
+
+            prod = work.tile([P, N], F32, name="prod")
+            nc.vector.tensor_tensor(prod[:], x_sb[b][:].indirect(offsets[:]), scale[:], MULT)
+
+            res = work.tile([P, N], F32, name="res")
+            nc.vector.tensor_tensor(res[:], prod[:], tr[:], ADD)
+
+            nc.sync.dma_start(out_blocks[b], res[:])

@@ -23,31 +23,36 @@ def tile_affine_coupling_layer_kernel(tc, x, hid, w_s, w_t, offs, out):
         offsets = held.tile([P, N // 16], U16, name="offsets")
         nc.sync.dma_start(offsets[:], offs)
 
-        ws_sb = held.tile([P, KSTEPS, N], BF16, name="ws_sb")
-        wt_sb = held.tile([P, KSTEPS, N], BF16, name="wt_sb")
-        hid_sb = held.tile([P, KSTEPS, C], BF16, name="hid_sb")
-        nc.scalar.dma_start(hid_sb[:], hid.rearrange("(k p) c -> p k c", p=P))
-        nc.sync.dma_start(ws_sb[:], w_s.rearrange("(k p) n -> p k n", p=P))
-        nc.scalar.dma_start(wt_sb[:], w_t.rearrange("(k p) n -> p k n", p=P))
-
+        hid_blocks = hid.rearrange("(k p) (b c) -> b p k c", p=P, c=P)
         x_blocks = x.rearrange("(b p) s -> b p s", p=P)
         out_blocks = out.rearrange("(b p) n -> b p n", p=P)
+
+        ws_sb = held.tile([P, KSTEPS, N], BF16, name="ws_sb")
+        wt_sb = held.tile([P, KSTEPS, N], BF16, name="wt_sb")
+        nc.sync.dma_start(ws_sb[:], w_s.rearrange("(k p) n -> p k n", p=P))
+
+        hid_sb = []
         x_sb = []
         for b in range(BLOCKS):
+            hid_b = held.tile([P, KSTEPS, P], BF16, name=f"hid{b}")
             x_b = held.tile([P, S], F32, name=f"x{b}")
+            if b == 0:
+                nc.scalar.dma_start(hid_b[:], hid_blocks[b])
+                nc.scalar.dma_start(wt_sb[:], w_t.rearrange("(k p) n -> p k n", p=P))
+            else:
+                nc.sync.dma_start(hid_b[:], hid_blocks[b])
             nc.sync.dma_start(x_b[:], x_blocks[b])
+            hid_sb.append(hid_b)
             x_sb.append(x_b)
 
         for b in range(BLOCKS):
-            samples = slice(b * P, (b + 1) * P)
-
             sc = psum.tile([P, N], F32, name="sc")
             tr = psum.tile([P, N], F32, name="tr")
             for acc, w_sb in ((sc, ws_sb), (tr, wt_sb)):
                 for k in range(KSTEPS):
                     nc.tensor.matmul(
                         acc[:],
-                        hid_sb[:, k, samples],
+                        hid_sb[b][:, k, :],
                         w_sb[:, k, :],
                         start=(k == 0),
                         stop=(k == KSTEPS - 1),

@@ -45,26 +45,31 @@ def tile_affine_coupling_layer_kernel(tc, x, hid, w_s, w_t, offs, out):
             hid_sb.append(hid_b)
             x_sb.append(x_b)
 
-        for b in range(BLOCKS):
-            sc = psum.tile([P, N], F32, name="sc")
-            tr = psum.tile([P, N], F32, name="tr")
-            for acc, w_sb in ((sc, ws_sb), (tr, wt_sb)):
-                for k in range(KSTEPS):
-                    nc.tensor.matmul(
-                        acc[:],
-                        hid_sb[b][:, k, :],
-                        w_sb[:, k, :],
-                        start=(k == 0),
-                        stop=(k == KSTEPS - 1),
-                    )
+        prods = []
+        trs = []
+        for b in range(BLOCKS + 1):
+            if b < BLOCKS:
+                sc = psum.tile([P, N], F32, name="sc")
+                tr = psum.tile([P, N], F32, name="tr")
+                for acc, w_sb in ((sc, ws_sb), (tr, wt_sb)):
+                    for k in range(KSTEPS):
+                        nc.tensor.matmul(
+                            acc[:],
+                            hid_sb[b][:, k, :],
+                            w_sb[:, k, :],
+                            start=(k == 0),
+                            stop=(k == KSTEPS - 1),
+                        )
 
-            scale = work.tile([P, N], F32, name="scale")
-            nc.scalar.activation(scale[:], sc[:], EXP)
+                scale = work.tile([P, N], F32, name="scale")
+                nc.scalar.activation(scale[:], sc[:], EXP)
 
-            prod = work.tile([P, N], F32, name="prod")
-            nc.vector.tensor_tensor(prod[:], x_sb[b][:].indirect(offsets[:]), scale[:], MULT)
+                prod = work.tile([P, N], F32, name="prod")
+                nc.vector.tensor_tensor(prod[:], x_sb[b][:].indirect(offsets[:]), scale[:], MULT)
+                prods.append(prod)
+                trs.append(tr)
 
-            res = work.tile([P, N], F32, name="res")
-            nc.vector.tensor_tensor(res[:], prod[:], tr[:], ADD)
-
-            nc.sync.dma_start(out_blocks[b], res[:])
+            if b > 0:
+                res = work.tile([P, N], F32, name="res")
+                nc.vector.tensor_tensor(res[:], prods[b - 1][:], trs[b - 1][:], ADD)
+                nc.sync.dma_start(out_blocks[b - 1], res[:])

@@ -4,6 +4,7 @@ P = 128
 C, S, N, H = 1024, 512, 384, 256
 BLOCKS = C // P
 KSTEPS = H // P
+HID_PIECE = 2
 
 BF16, F32, U16 = mybir.dt.bfloat16, mybir.dt.float32, mybir.dt.uint16
 MULT, ADD = mybir.AluOpType.mult, mybir.AluOpType.add
@@ -23,53 +24,50 @@ def tile_affine_coupling_layer_kernel(tc, x, hid, w_s, w_t, offs, out):
         offsets = held.tile([P, N // 16], U16, name="offsets")
         nc.sync.dma_start(offsets[:], offs)
 
-        hid_blocks = hid.rearrange("(k p) (b c) -> b p k c", p=P, c=P)
+        hid_pieces = hid.rearrange("(k p) (g c) -> g p k c", p=P, c=HID_PIECE * P)
         x_blocks = x.rearrange("(b p) s -> b p s", p=P)
         out_blocks = out.rearrange("(b p) n -> b p n", p=P)
 
         ws_sb = held.tile([P, KSTEPS, N], BF16, name="ws_sb")
         wt_sb = held.tile([P, KSTEPS, N], BF16, name="wt_sb")
+        hid_sb = [
+            held.tile([P, KSTEPS, HID_PIECE * P], BF16, name=f"hid{g}")
+            for g in range(BLOCKS // HID_PIECE)
+        ]
+        x_sb = [held.tile([P, S], F32, name=f"x{b}") for b in range(BLOCKS)]
+
         nc.sync.dma_start(ws_sb[:], w_s.rearrange("(k p) n -> p k n", p=P))
-
-        hid_sb = []
-        x_sb = []
+        nc.sync.dma_start(hid_sb[0][:], hid_pieces[0])
         for b in range(BLOCKS):
-            hid_b = held.tile([P, KSTEPS, P], BF16, name=f"hid{b}")
-            x_b = held.tile([P, S], F32, name=f"x{b}")
+            if (b + 1) % HID_PIECE == 0 and b + 1 < BLOCKS:
+                nc.sync.dma_start(hid_sb[(b + 1) // HID_PIECE][:], hid_pieces[(b + 1) // HID_PIECE])
+            nc.sync.dma_start(x_sb[b][:], x_blocks[b])
             if b == 0:
-                nc.scalar.dma_start(hid_b[:], hid_blocks[b])
-                nc.scalar.dma_start(wt_sb[:], w_t.rearrange("(k p) n -> p k n", p=P))
-            else:
-                nc.sync.dma_start(hid_b[:], hid_blocks[b])
-            nc.sync.dma_start(x_b[:], x_blocks[b])
-            hid_sb.append(hid_b)
-            x_sb.append(x_b)
+                nc.sync.dma_start(wt_sb[:], w_t.rearrange("(k p) n -> p k n", p=P))
 
-        prods = []
-        trs = []
-        for b in range(BLOCKS + 1):
-            if b < BLOCKS:
-                sc = psum.tile([P, N], F32, name="sc")
-                tr = psum.tile([P, N], F32, name="tr")
-                for acc, w_sb in ((sc, ws_sb), (tr, wt_sb)):
-                    for k in range(KSTEPS):
-                        nc.tensor.matmul(
-                            acc[:],
-                            hid_sb[b][:, k, :],
-                            w_sb[:, k, :],
-                            start=(k == 0),
-                            stop=(k == KSTEPS - 1),
-                        )
+        for b in range(BLOCKS):
+            hid_b = hid_sb[b // HID_PIECE]
+            samples = slice((b % HID_PIECE) * P, (b % HID_PIECE + 1) * P)
 
-                scale = work.tile([P, N], F32, name="scale")
-                nc.scalar.activation(scale[:], sc[:], EXP)
+            sc = psum.tile([P, N], F32, name="sc")
+            tr = psum.tile([P, N], F32, name="tr")
+            for acc, w_sb in ((sc, ws_sb), (tr, wt_sb)):
+                for k in range(KSTEPS):
+                    nc.tensor.matmul(
+                        acc[:],
+                        hid_b[:, k, samples],
+                        w_sb[:, k, :],
+                        start=(k == 0),
+                        stop=(k == KSTEPS - 1),
+                    )
 
-                prod = work.tile([P, N], F32, name="prod")
-                nc.vector.tensor_tensor(prod[:], x_sb[b][:].indirect(offsets[:]), scale[:], MULT)
-                prods.append(prod)
-                trs.append(tr)
+            scale = work.tile([P, N], F32, name="scale")
+            nc.scalar.activation(scale[:], sc[:], EXP)
 
-            if b > 0:
-                res = work.tile([P, N], F32, name="res")
-                nc.vector.tensor_tensor(res[:], prods[b - 1][:], trs[b - 1][:], ADD)
-                nc.sync.dma_start(out_blocks[b - 1], res[:])
+            prod = work.tile([P, N], F32, name="prod")
+            nc.vector.tensor_tensor(prod[:], x_sb[b][:].indirect(offsets[:]), scale[:], MULT)
+
+            res = work.tile([P, N], F32, name="res")
+            nc.vector.tensor_tensor(res[:], prod[:], tr[:], ADD)
+
+            nc.sync.dma_start(out_blocks[b], res[:])

@@ -1,10 +1,13 @@
 import concourse.mybir as mybir
+from concourse.masks import make_identity
 
 P = 128
 C, S, N, H = 1024, 512, 384, 256
 BLOCKS = C // P
 KSTEPS = H // P
 HID_PIECE = 2
+AHEAD = 3
+TENSOR_ADDS = range(BLOCKS - 4, BLOCKS - 1)
 
 BF16, F32, U16 = mybir.dt.bfloat16, mybir.dt.float32, mybir.dt.uint16
 MULT, ADD = mybir.AluOpType.mult, mybir.AluOpType.add
@@ -18,11 +21,11 @@ def tile_affine_coupling_layer_kernel(tc, x, hid, w_s, w_t, offs, out):
     nc = tc.nc
     with (
         tc.tile_pool(name="held", bufs=1) as held,
-        tc.tile_pool(name="work", bufs=3) as work,
-        tc.psum_pool(name="psum", bufs=4) as psum,
+        tc.tile_pool(name="work", bufs=AHEAD + 1) as work,
+        tc.psum_pool(name="psum_sc", bufs=3) as psum_sc,
+        tc.psum_pool(name="psum_tr", bufs=5) as psum_tr,
     ):
         offsets = held.tile([P, N // 16], U16, name="offsets")
-        nc.sync.dma_start(offsets[:], offs)
 
         hid_pieces = hid.rearrange("(k p) (g c) -> g p k c", p=P, c=HID_PIECE * P)
         x_blocks = x.rearrange("(b p) s -> b p s", p=P)
@@ -36,38 +39,60 @@ def tile_affine_coupling_layer_kernel(tc, x, hid, w_s, w_t, offs, out):
         ]
         x_sb = [held.tile([P, S], F32, name=f"x{b}") for b in range(BLOCKS)]
 
-        nc.sync.dma_start(ws_sb[:], w_s.rearrange("(k p) n -> p k n", p=P))
         nc.sync.dma_start(hid_sb[0][:], hid_pieces[0])
+        nc.sync.dma_start(ws_sb[:], w_s.rearrange("(k p) n -> p k n", p=P))
         for b in range(BLOCKS):
             if (b + 1) % HID_PIECE == 0 and b + 1 < BLOCKS:
                 nc.sync.dma_start(hid_sb[(b + 1) // HID_PIECE][:], hid_pieces[(b + 1) // HID_PIECE])
             nc.sync.dma_start(x_sb[b][:], x_blocks[b])
             if b == 0:
+                nc.sync.dma_start(offsets[:], offs)
                 nc.sync.dma_start(wt_sb[:], w_t.rearrange("(k p) n -> p k n", p=P))
 
-        for b in range(BLOCKS):
+        ident = held.tile([P, P], F32, name="ident")
+        make_identity(nc, ident[:])
+
+        scales = {}
+        translations = {}
+
+        def read_outs(b):
             hid_b = hid_sb[b // HID_PIECE]
             samples = slice((b % HID_PIECE) * P, (b % HID_PIECE + 1) * P)
-
-            sc = psum.tile([P, N], F32, name="sc")
-            tr = psum.tile([P, N], F32, name="tr")
-            for acc, w_sb in ((sc, ws_sb), (tr, wt_sb)):
-                for k in range(KSTEPS):
-                    nc.tensor.matmul(
-                        acc[:],
-                        hid_b[:, k, samples],
-                        w_sb[:, k, :],
-                        start=(k == 0),
-                        stop=(k == KSTEPS - 1),
-                    )
-
+            sc = psum_sc.tile([P, N], F32, name="sc")
+            tr = psum_tr.tile([P, N], F32, name="tr")
+            for k in range(KSTEPS):
+                nc.tensor.matmul(
+                    sc[:], hid_b[:, k, samples], ws_sb[:, k, :], start=(k == 0), stop=(k == KSTEPS - 1)
+                )
+            for k in range(KSTEPS):
+                nc.tensor.matmul(
+                    tr[:],
+                    hid_b[:, k, samples],
+                    wt_sb[:, k, :],
+                    start=(k == 0),
+                    stop=(k == KSTEPS - 1 and b not in TENSOR_ADDS),
+                )
             scale = work.tile([P, N], F32, name="scale")
             nc.scalar.activation(scale[:], sc[:], EXP)
+            scales[b] = scale
+            translations[b] = tr
+
+        for b in range(AHEAD):
+            read_outs(b)
+
+        for b in range(BLOCKS):
+            if b + AHEAD < BLOCKS:
+                read_outs(b + AHEAD)
+            tr = translations[b]
 
             prod = work.tile([P, N], F32, name="prod")
-            nc.vector.tensor_tensor(prod[:], x_sb[b][:].indirect(offsets[:]), scale[:], MULT)
+            nc.vector.tensor_tensor(prod[:], x_sb[b][:].indirect(offsets[:]), scales[b][:], MULT)
 
             res = work.tile([P, N], F32, name="res")
-            nc.vector.tensor_tensor(res[:], prod[:], tr[:], ADD)
+            if b in TENSOR_ADDS:
+                nc.tensor.matmul(tr[:], ident[:], prod[:], start=False, stop=True)
+                nc.scalar.copy(res[:], tr[:])
+            else:
+                nc.vector.tensor_tensor(res[:], prod[:], tr[:], ADD)
 
             nc.sync.dma_start(out_blocks[b], res[:])

@@ -92,7 +92,7 @@ def tile_affine_coupling_layer_kernel(tc, x, hid, w_s, w_t, offs, out):
             if b in TENSOR_ADDS:
                 nc.tensor.matmul(tr[:], ident[:], prod[:], start=False, stop=True)
                 nc.scalar.copy(res[:], tr[:])
+                nc.scalar.dma_start(out_blocks[b], res[:])
             else:
                 nc.vector.tensor_tensor(res[:], prod[:], tr[:], ADD)
-
-            nc.sync.dma_start(out_blocks[b], res[:])
+                nc.sync.dma_start(out_blocks[b], res[:])

@@ -6,7 +6,8 @@ C, S, N, H = 1024, 512, 384, 256
 BLOCKS = C // P
 KSTEPS = H // P
 HID_PIECE = 2
-AHEAD = 3
+TR_AHEAD = 3
+SC_AHEAD = TR_AHEAD + 1
 TENSOR_ADDS = range(BLOCKS - 4, BLOCKS - 1)
 
 BF16, F32, U16 = mybir.dt.bfloat16, mybir.dt.float32, mybir.dt.uint16
@@ -21,7 +22,7 @@ def tile_affine_coupling_layer_kernel(tc, x, hid, w_s, w_t, offs, out):
     nc = tc.nc
     with (
         tc.tile_pool(name="held", bufs=1) as held,
-        tc.tile_pool(name="work", bufs=AHEAD + 1) as work,
+        tc.tile_pool(name="work", bufs=SC_AHEAD + 1) as work,
         tc.psum_pool(name="psum_sc", bufs=3) as psum_sc,
         tc.psum_pool(name="psum_tr", bufs=5) as psum_tr,
     ):
@@ -42,12 +43,13 @@ def tile_affine_coupling_layer_kernel(tc, x, hid, w_s, w_t, offs, out):
         nc.sync.dma_start(hid_sb[0][:], hid_pieces[0])
         nc.sync.dma_start(ws_sb[:], w_s.rearrange("(k p) n -> p k n", p=P))
         for b in range(BLOCKS):
-            if (b + 1) % HID_PIECE == 0 and b + 1 < BLOCKS:
-                nc.sync.dma_start(hid_sb[(b + 1) // HID_PIECE][:], hid_pieces[(b + 1) // HID_PIECE])
             nc.sync.dma_start(x_sb[b][:], x_blocks[b])
             if b == 0:
                 nc.sync.dma_start(offsets[:], offs)
                 nc.sync.dma_start(wt_sb[:], w_t.rearrange("(k p) n -> p k n", p=P))
+            ahead = b + 2
+            if ahead % HID_PIECE == 0 and ahead < BLOCKS:
+                nc.sync.dma_start(hid_sb[ahead // HID_PIECE][:], hid_pieces[ahead // HID_PIECE])
 
         ident = held.tile([P, P], F32, name="ident")
         make_identity(nc, ident[:])
@@ -55,34 +57,44 @@ def tile_affine_coupling_layer_kernel(tc, x, hid, w_s, w_t, offs, out):
         scales = {}
         translations = {}
 
-        def read_outs(b):
-            hid_b = hid_sb[b // HID_PIECE]
-            samples = slice((b % HID_PIECE) * P, (b % HID_PIECE + 1) * P)
+        def hid_of(b, k):
+            first = (b % HID_PIECE) * P
+            return hid_sb[b // HID_PIECE][:, k, first : first + P]
+
+        def logits(b):
             sc = psum_sc.tile([P, N], F32, name="sc")
-            tr = psum_tr.tile([P, N], F32, name="tr")
             for k in range(KSTEPS):
                 nc.tensor.matmul(
-                    sc[:], hid_b[:, k, samples], ws_sb[:, k, :], start=(k == 0), stop=(k == KSTEPS - 1)
-                )
-            for k in range(KSTEPS):
-                nc.tensor.matmul(
-                    tr[:],
-                    hid_b[:, k, samples],
-                    wt_sb[:, k, :],
-                    start=(k == 0),
-                    stop=(k == KSTEPS - 1 and b not in TENSOR_ADDS),
+                    sc[:], hid_of(b, k), ws_sb[:, k, :], start=(k == 0), stop=(k == KSTEPS - 1)
                 )
             scale = work.tile([P, N], F32, name="scale")
             nc.scalar.activation(scale[:], sc[:], EXP)
             scales[b] = scale
+
+        def translation(b):
+            tr = psum_tr.tile([P, N], F32, name="tr")
+            for k in range(KSTEPS):
+                nc.tensor.matmul(
+                    tr[:],
+                    hid_of(b, k),
+                    wt_sb[:, k, :],
+                    start=(k == 0),
+                    stop=(k == KSTEPS - 1 and b not in TENSOR_ADDS),
+                )
             translations[b] = tr
 
-        for b in range(AHEAD):
+        def read_outs(b):
+            if b + 1 < BLOCKS:
+                logits(b + 1)
+            translation(b)
+
+        logits(0)
+        for b in range(TR_AHEAD):
             read_outs(b)
 
         for b in range(BLOCKS):
-            if b + AHEAD < BLOCKS:
-                read_outs(b + AHEAD)
+            if b + TR_AHEAD < BLOCKS:
+                read_outs(b + TR_AHEAD)
             tr = translations[b]
 
             prod = work.tile([P, N], F32, name="prod")

@@ -81,7 +81,12 @@ def tile_affine_coupling_layer_kernel(tc, x, hid, w_s, w_t, offs, out):
                     start=(k == 0),
                     stop=(k == KSTEPS - 1 and b not in TENSOR_ADDS),
                 )
-            translations[b] = tr
+            if b in TENSOR_ADDS:
+                translations[b] = tr
+            else:
+                tr_sb = work.tile([P, N], F32, name="tr_sb")
+                nc.scalar.copy(tr_sb[:], tr[:])
+                translations[b] = tr_sb
 
         def read_outs(b):
             if b + 1 < BLOCKS:

import concourse.mybir as mybir
from concourse.masks import make_identity

P = 128
C, S, N, H = 1024, 512, 384, 256
BLOCKS = C // P
KSTEPS = H // P
HID_PIECE = 2
TR_AHEAD = 3
SC_AHEAD = TR_AHEAD + 1
TENSOR_ADDS = range(BLOCKS - 4, BLOCKS - 1)

BF16, F32, U16 = mybir.dt.bfloat16, mybir.dt.float32, mybir.dt.uint16
MULT, ADD = mybir.AluOpType.mult, mybir.AluOpType.add
EXP = mybir.ActivationFunctionType.Exp

FLOPS = 2 * 2 * C * H * N
BYTES = 4 * C * N + 2 * H * C + 2 * 2 * H * N + 2 * P * (N // 16) + 4 * C * N


def tile_affine_coupling_layer_kernel(tc, x, hid, w_s, w_t, offs, out):
    nc = tc.nc
    with (
        tc.tile_pool(name="held", bufs=1) as held,
        tc.tile_pool(name="work", bufs=SC_AHEAD + 1) as work,
        tc.psum_pool(name="psum_sc", bufs=3) as psum_sc,
        tc.psum_pool(name="psum_tr", bufs=5) as psum_tr,
    ):
        offsets = held.tile([P, N // 16], U16, name="offsets")

        hid_pieces = hid.rearrange("(k p) (g c) -> g p k c", p=P, c=HID_PIECE * P)
        x_blocks = x.rearrange("(b p) s -> b p s", p=P)
        out_blocks = out.rearrange("(b p) n -> b p n", p=P)

        ws_sb = held.tile([P, KSTEPS, N], BF16, name="ws_sb")
        wt_sb = held.tile([P, KSTEPS, N], BF16, name="wt_sb")
        hid_sb = [
            held.tile([P, KSTEPS, HID_PIECE * P], BF16, name=f"hid{g}")
            for g in range(BLOCKS // HID_PIECE)
        ]
        x_sb = [held.tile([P, S], F32, name=f"x{b}") for b in range(BLOCKS)]

        nc.sync.dma_start(hid_sb[0][:], hid_pieces[0])
        nc.sync.dma_start(ws_sb[:], w_s.rearrange("(k p) n -> p k n", p=P))
        for b in range(BLOCKS):
            nc.sync.dma_start(x_sb[b][:], x_blocks[b])
            if b == 0:
                nc.sync.dma_start(offsets[:], offs)
                nc.sync.dma_start(wt_sb[:], w_t.rearrange("(k p) n -> p k n", p=P))
            ahead = b + 2
            if ahead % HID_PIECE == 0 and ahead < BLOCKS:
                nc.sync.dma_start(hid_sb[ahead // HID_PIECE][:], hid_pieces[ahead // HID_PIECE])

        ident = held.tile([P, P], F32, name="ident")
        make_identity(nc, ident[:])

        scales = {}
        translations = {}

        def hid_of(b, k):
            first = (b % HID_PIECE) * P
            return hid_sb[b // HID_PIECE][:, k, first : first + P]

        def logits(b):
            sc = psum_sc.tile([P, N], F32, name="sc")
            for k in range(KSTEPS):
                nc.tensor.matmul(
                    sc[:], hid_of(b, k), ws_sb[:, k, :], start=(k == 0), stop=(k == KSTEPS - 1)
                )
            scale = work.tile([P, N], F32, name="scale")
            nc.scalar.activation(scale[:], sc[:], EXP)
            scales[b] = scale

        def translation(b):
            tr = psum_tr.tile([P, N], F32, name="tr")
            for k in range(KSTEPS):
                nc.tensor.matmul(
                    tr[:],
                    hid_of(b, k),
                    wt_sb[:, k, :],
                    start=(k == 0),
                    stop=(k == KSTEPS - 1 and b not in TENSOR_ADDS),
                )
            if b in TENSOR_ADDS:
                translations[b] = tr
            else:
                tr_sb = work.tile([P, N], F32, name="tr_sb")
                nc.scalar.copy(tr_sb[:], tr[:])
                translations[b] = tr_sb

        def read_outs(b):
            if b + 1 < BLOCKS:
                logits(b + 1)
            translation(b)

        logits(0)
        for b in range(TR_AHEAD):
            read_outs(b)

        for b in range(BLOCKS):
            if b + TR_AHEAD < BLOCKS:
                read_outs(b + TR_AHEAD)
            tr = translations[b]

            prod = work.tile([P, N], F32, name="prod")
            nc.vector.tensor_tensor(prod[:], x_sb[b][:].indirect(offsets[:]), scales[b][:], MULT)

            res = work.tile([P, N], F32, name="res")
            if b in TENSOR_ADDS:
                nc.tensor.matmul(tr[:], ident[:], prod[:], start=False, stop=True)
                nc.scalar.copy(res[:], tr[:])
                nc.scalar.dma_start(out_blocks[b], res[:])
            else:
                nc.vector.tensor_tensor(res[:], prod[:], tr[:], ADD)
                nc.sync.dma_start(out_blocks[b], res[:])
